import numpy as np
import ml_dtypes


def mxq(x, axis, fmt="e4m3"):
    dtype, down = {"e4m3": (ml_dtypes.float8_e4m3fn, 7), "e5m2": (ml_dtypes.float8_e5m2, 14)}[fmt]
    v = np.moveaxis(np.asarray(x, np.float32).astype(ml_dtypes.bfloat16).astype(np.float64), axis, -1)
    blocks = v.reshape(v.shape[:-1] + (-1, 32))
    amax = np.abs(blocks).max(-1, keepdims=True)
    byte = np.maximum(np.where(amax > 0, np.frexp(amax)[1] - 1 + 127, 0) - down, 1)
    scale = np.exp2(byte - 127.0)
    codes = (blocks / scale).astype(np.float32).astype(dtype).astype(np.float64)
    return np.moveaxis((codes * scale).reshape(v.shape), -1, axis)


WIDE = False


def mx_kscale(k):
    if not WIDE:
        return np.ones(k)
    levels = np.array([10, -10, 5, -5, 0])
    a = np.random.permutation(np.resize(levels, k // 512 * 4)).reshape(k // 512, 4)
    idx = np.arange(k)
    return np.exp2(a[idx // 512, idx % 128 // 32])


BF16 = ml_dtypes.bfloat16


def bf(x):
    return np.asarray(x, np.float32).astype(BF16)


def f64(x):
    return np.asarray(x).astype(np.float64)


B, S, DIM, H, NOPE, ROPE, VD = 4, 1024, 1024, 4, 192, 64, 128
QK = NOPE + ROPE


def apply_rope(t, freqs):
    b, s, h, d = t.shape
    tr = t.reshape(b, s, h, d // 2, 2)
    cos = np.cos(freqs)[None, :, None, :]
    sin = np.sin(freqs)[None, :, None, :]
    out = np.stack([tr[..., 0] * cos - tr[..., 1] * sin,
                    tr[..., 0] * sin + tr[..., 1] * cos], axis=-1)
    return out.reshape(b, s, h, d)


def setup_inputs():
    s = mx_kscale(DIM)
    inv_freq = 1.0 / (10000.0 ** (np.arange(0, ROPE, 2) / ROPE))
    ang = np.arange(S)[:, None] * inv_freq[None, :]
    ang = ang - 2.0 * np.pi * np.round(ang / (2.0 * np.pi))
    return {"x": bf(np.random.standard_normal((B, S, DIM)) * s),
            "w": bf(np.random.standard_normal((DIM, H * QK)) / np.sqrt(DIM) / s[:, None]),
            "freqs": bf(ang)}


def reference(x, w, freqs):
    y = mxq(f64(x), 2, "e4m3") @ mxq(f64(w), 0, "e4m3")
    nope = y[..., :H * NOPE].reshape(B, S, H, NOPE)
    rope = apply_rope(y[..., H * NOPE:].reshape(B, S, H, ROPE), f64(freqs))
    return np.concatenate([nope, rope], axis=-1)

@@ -1,0 +1,254 @@
+from contextlib import ExitStack
+
+import concourse.mybir as mybir
+from concourse.masks import make_identity
+
+BF16 = mybir.dt.bfloat16
+F32 = mybir.dt.float32
+U32 = mybir.dt.uint32
+U8 = mybir.dt.uint8
+FP8X4 = mybir.dt.float8_e4m3fn_x4
+ACT = mybir.ActivationFunctionType
+ALU = mybir.AluOpType
+
+P = 128
+PACK = 4
+BATCH, SEQ, DIM = 4, 1024, 1024
+HEADS, NOPE, ROPE = 4, 192, 64
+QK = NOPE + ROPE
+PASSES = DIM // (P * PACK)
+TILES = SEQ // P
+PAIR = 2
+PAIRS_PER_BATCH = TILES // PAIR
+PAIRS = BATCH * PAIRS_PER_BATCH
+PART = 64
+CHUNKS = QK // PART
+CHUNK_COLS = HEADS * PART
+ROPE_CHUNK = CHUNKS - 1
+CHUNK_ORDER = (ROPE_CHUNK, 0, 1, 2)
+BANK = 512
+AHEAD = 2
+
+FLOPS = 2 * BATCH * SEQ * DIM * HEADS * QK
+
+
+def tile_mla_pa_t_kernel(tc, x, w, freqs, out):
+    nc = tc.nc
+    x_rows = x.rearrange("b (p i) k -> b p (i k)", i=TILES)
+    out_rows = out.rearrange("b (p i) h d -> b p (i h d)", i=TILES)
+
+    with ExitStack() as ctx:
+        const = ctx.enter_context(tc.tile_pool(name="const", bufs=1))
+        x_pool = ctx.enter_context(tc.tile_pool(name="x_pool", bufs=PAIRS))
+        grouped_pool = ctx.enter_context(tc.tile_pool(name="grouped_pool", bufs=3))
+        code_pool = ctx.enter_context(tc.tile_pool(name="code_pool", bufs=AHEAD + 2))
+        term_pool = ctx.enter_context(tc.tile_pool(name="term_pool", bufs=2))
+        out_pool = ctx.enter_context(tc.tile_pool(name="out_pool", bufs=6))
+        xt_pool = ctx.enter_context(tc.psum_pool(name="xt_pool", bufs=4))
+        acc_pool = ctx.enter_context(tc.psum_pool(name="acc_pool", bufs=4))
+        ctx.enter_context(tc.manual_schedule())
+
+        angles = const.tile([P, TILES * ROPE // 2], BF16)
+        nc.scalar.dma_start(out=angles[:], in_=freqs.rearrange("(p i) j -> p (i j)", i=TILES))
+
+        w_raw = const.tile([P, PASSES, PACK, DIM], BF16)
+
+        def load_w(g):
+            rows = w[g * P * PACK : (g + 1) * P * PACK, :]
+            nc.sync.dma_start(
+                out=w_raw[:, g].rearrange("p (u e) n -> p u (e n)", u=2),
+                in_=rows.rearrange("(u p e) n -> p u (e n)", u=2, e=2),
+            )
+
+        x_tiles = {}
+
+        def load_x(r):
+            b, q = divmod(r, PAIRS_PER_BATCH)
+            x_sb = x_pool.tile([P, PAIR * DIM], BF16)
+            nc.sync.dma_start(out=x_sb[:], in_=x_rows[b, :, q * PAIR * DIM : (q + 1) * PAIR * DIM])
+            x_tiles[r] = x_sb
+
+        load_w(0)
+        load_x(0)
+        load_w(1)
+        for r in range(1, PAIRS):
+            load_x(r)
+
+        ident = const.tile([P, P], F32)
+        make_identity(nc, ident[:])
+
+        u_table = const.tile([P, TILES, ROPE], F32)
+        v_table = const.tile([P, TILES, ROPE], F32)
+        u_cols = u_table[:].rearrange("p i (j e) -> p (i j) e", e=2)
+        v_cols = v_table[:].rearrange("p i (j e) -> p (i j) e", e=2)
+        half_sin = const.tile([P, TILES * ROPE // 2], F32)
+        half_sq = const.tile([P, TILES * ROPE // 2], F32)
+        nc.scalar.activation(out=half_sin[:], in_=angles[:], func=ACT.Sin, scale=0.5)
+        nc.scalar.activation(out=u_cols[:, :, 1], in_=angles[:], func=ACT.Sin)
+        nc.scalar.activation(out=v_cols[:, :, 0], in_=angles[:], func=ACT.Sin, scale=-1.0)
+        nc.scalar.activation(out=half_sq[:], in_=half_sin[:], func=ACT.Square)
+        nc.scalar.activation(out=u_cols[:, :, 0], in_=half_sq[:], func=ACT.Copy, scale=-2.0, bias=1.0)
+        nc.scalar.activation(out=v_cols[:, :, 1], in_=half_sq[:], func=ACT.Copy, scale=-2.0, bias=1.0)
+
+        xt_banks = {}
+        grouped_tiles = {}
+        x_codes = {}
+        x_scales = {}
+
+        def transpose_pair(r):
+            words = x_tiles[r][:].bitcast(F32)
+            xt_banks[r] = []
+            for t in range(PAIR):
+                xt = xt_pool.tile([P, BANK], F32)
+                for s in range(PACK):
+                    col = (t * PACK + s) * P
+                    nc.tensor.transpose(
+                        out=xt[:, s * P : (s + 1) * P], in_=words[:, col : col + P], identity=ident[:]
+                    )
+                xt_banks[r].append(xt)
+
+        def group_pair(r):
+            grouped = grouped_pool.tile([P, PAIR * DIM], BF16, align_bytes=64)
+            grouped_words = grouped[:].bitcast(F32)
+            for t in range(PAIR):
+                nc.scalar.copy(
+                    out=grouped_words[:, t * BANK : (t + 1) * BANK].rearrange(
+                        "p (g k u) -> p g k u", g=PASSES, u=2
+                    ),
+                    in_=xt_banks[r][t][:].rearrange("p (g u k) -> p g k u", g=PASSES, u=2),
+                )
+            grouped_tiles[r] = grouped
+
+        def quantise_pair(r):
+            codes = code_pool.tile([P, PAIR * PASSES * P], U32, align_bytes=64)
+            scales = code_pool.tile([P, PAIR * PASSES * P], U8, align_bytes=64)
+            nc.vector.quantize_mx(
+                out=codes[:].bitcast(FP8X4), scales=scales[:], in_=grouped_tiles[r][:]
+            )
+            x_codes[r] = codes
+            x_scales[r] = scales
+
+        w_grouped = const.tile([P, PASSES, CHUNKS, CHUNK_COLS * PACK], BF16, align_bytes=64)
+        w_codes = const.tile([P, PASSES, CHUNKS * CHUNK_COLS], U32, align_bytes=64)
+        w_scales = const.tile([P, PASSES, CHUNKS * CHUNK_COLS], U8, align_bytes=64)
+
+        def group_w(g, c, on_scalar):
+            if c == ROPE_CHUNK:
+                src = w_raw[:, g, :, HEADS * NOPE :].rearrange("p t (h n) -> p h n t", h=HEADS)
+            else:
+                src = w_raw[:, g, :, : HEADS * NOPE].rearrange(
+                    "p t (h c n) -> p c h n t", h=HEADS, n=PART
+                )[:, c]
+            dst = w_grouped[:, g, c, :].rearrange("p (h n t) -> p h n t", h=HEADS, t=PACK)
+            if on_scalar:
+                nc.scalar.copy(out=dst, in_=src)
+            else:
+                nc.vector.tensor_copy(out=dst, in_=src)
+
+        def quantise_w(g, c):
+            cols = slice(c * CHUNK_COLS, (c + 1) * CHUNK_COLS)
+            nc.vector.quantize_mx(
+                out=w_codes[:, g, cols].bitcast(FP8X4),
+                scales=w_scales[:, g, cols],
+                in_=w_grouped[:, g, c, :],
+            )
+
+        def prepare_w(g, share_with_scalar):
+            for n, c in enumerate(CHUNK_ORDER):
+                group_w(g, c, on_scalar=share_with_scalar and n % 2 == 1)
+                if n > 0:
+                    quantise_w(g, CHUNK_ORDER[n - 1])
+            quantise_w(g, CHUNK_ORDER[-1])
+
+        acc_banks = {}
+        out_tiles = {}
+
+        def multiply_pair(r):
+            for c in CHUNK_ORDER:
+                acc = acc_pool.tile([P, BANK], F32)
+                w_cols = slice(c * CHUNK_COLS, (c + 1) * CHUNK_COLS)
+                for t in range(PAIR):
+                    for g in range(PASSES):
+                        x_cols = slice((t * PASSES + g) * P, (t * PASSES + g + 1) * P)
+                        nc.tensor.matmul_mx(
+                            out=acc[:, t * CHUNK_COLS : (t + 1) * CHUNK_COLS],
+                            lhsT=x_codes[r][:, x_cols].bitcast(FP8X4),
+                            lhsT_scale=x_scales[r][:, x_cols],
+                            rhs=w_codes[:, g, w_cols].bitcast(FP8X4),
+                            rhs_scale=w_scales[:, g, w_cols],
+                            start=(g == 0),
+                            stop=(g == PASSES - 1),
+                        )
+                acc_banks[r, c] = acc
+
+        full = [P, PAIR, HEADS, ROPE // 2, 2]
+        split = "p (t h j e) -> p t h j e"
+
+        def rotate_products(r):
+            i0 = (r % PAIRS_PER_BATCH) * PAIR
+            pairs = acc_banks[r, ROPE_CHUNK][:].rearrange(split, t=PAIR, h=HEADS, e=2)
+            terms = []
+            for e, table in enumerate((u_table, v_table)):
+                term = term_pool.tile([P, BANK], F32, name="term%d" % e)
+                nc.vector.tensor_tensor(
+                    out=term[:].rearrange(split, t=PAIR, h=HEADS, e=2),
+                    in0=pairs[:, :, :, :, e : e + 1].to_broadcast(full),
+                    in1=table[:, i0 : i0 + PAIR, :]
+                    .rearrange("p t (j e) -> p t j e", e=2)
+                    .unsqueeze(2)
+                    .to_broadcast(full),
+                    op=ALU.mult,
+                )
+                terms.append(term)
+            return terms
+
+        def out_part(r, c):
+            view = out_tiles[r][:].rearrange("p (t h d) -> p t h d", t=PAIR, h=HEADS)
+            return view[:, :, :, c * PART : (c + 1) * PART]
+
+        by_head = "p (t h n) -> p t h n"
+
+        def rotate_sum(r, terms):
+            nc.vector.tensor_tensor(
+                out=out_part(r, ROPE_CHUNK),
+                in0=terms[0][:].rearrange(by_head, t=PAIR, h=HEADS),
+                in1=terms[1][:].rearrange(by_head, t=PAIR, h=HEADS),
+                op=ALU.add,
+            )
+
+        def copy_nope(r):
+            for c in range(ROPE_CHUNK):
+                nc.scalar.copy(
+                    out=out_part(r, c),
+                    in_=acc_banks[r, c][:].rearrange(by_head, t=PAIR, h=HEADS),
+                )
+
+        def store_pair(r):
+            b, q = divmod(r, PAIRS_PER_BATCH)
+            width = PAIR * HEADS * QK
+            nc.sync.dma_start(out=out_rows[b, :, q * width : (q + 1) * width], in_=out_tiles[r][:])
+
+        transpose_pair(0)
+        group_pair(0)
+        prepare_w(0, share_with_scalar=False)
+        quantise_pair(0)
+        prepare_w(1, share_with_scalar=True)
+        transpose_pair(1)
+        group_pair(1)
+        quantise_pair(1)
+
+        for r in range(PAIRS):
+            ahead = r + AHEAD
+            if ahead < PAIRS:
+                transpose_pair(ahead)
+            multiply_pair(r)
+            if ahead < PAIRS:
+                group_pair(ahead)
+            out_sb = out_pool.tile([P, PAIR * HEADS * QK], F32)
+            out_tiles[r] = out_sb
+            terms = rotate_products(r)
+            if ahead < PAIRS:
+                quantise_pair(ahead)
+            rotate_sum(r, terms)
+            copy_nope(r)
+            store_pair(r)

@@ -27,7 +27,7 @@ CHUNK_COLS = HEADS * PART
 ROPE_CHUNK = CHUNKS - 1
 CHUNK_ORDER = (ROPE_CHUNK, 0, 1, 2)
 BANK = 512
-AHEAD = 2
+ROUND = 2
 
 FLOPS = 2 * BATCH * SEQ * DIM * HEADS * QK
 
@@ -41,7 +41,7 @@ def tile_mla_pa_t_kernel(tc, x, w, freqs, out):
         const = ctx.enter_context(tc.tile_pool(name="const", bufs=1))
         x_pool = ctx.enter_context(tc.tile_pool(name="x_pool", bufs=PAIRS))
         grouped_pool = ctx.enter_context(tc.tile_pool(name="grouped_pool", bufs=3))
-        code_pool = ctx.enter_context(tc.tile_pool(name="code_pool", bufs=AHEAD + 2))
+        code_pool = ctx.enter_context(tc.tile_pool(name="code_pool", bufs=2 * ROUND))
         term_pool = ctx.enter_context(tc.tile_pool(name="term_pool", bufs=2))
         out_pool = ctx.enter_context(tc.tile_pool(name="out_pool", bufs=6))
         xt_pool = ctx.enter_context(tc.psum_pool(name="xt_pool", bufs=4))
@@ -228,27 +228,34 @@ def tile_mla_pa_t_kernel(tc, x, w, freqs, out):
             width = PAIR * HEADS * QK
             nc.sync.dma_start(out=out_rows[b, :, q * width : (q + 1) * width], in_=out_tiles[r][:])
 
+        def finish_pair(r, quantise_between):
+            out_sb = out_pool.tile([P, PAIR * HEADS * QK], F32)
+            out_tiles[r] = out_sb
+            terms = rotate_products(r)
+            if quantise_between is not None:
+                quantise_pair(quantise_between)
+            rotate_sum(r, terms)
+            copy_nope(r)
+            store_pair(r)
+
         transpose_pair(0)
         group_pair(0)
         prepare_w(0, share_with_scalar=False)
         quantise_pair(0)
         prepare_w(1, share_with_scalar=True)
         transpose_pair(1)
-        group_pair(1)
-        quantise_pair(1)
 
-        for r in range(PAIRS):
-            ahead = r + AHEAD
-            if ahead < PAIRS:
-                transpose_pair(ahead)
-            multiply_pair(r)
-            if ahead < PAIRS:
-                group_pair(ahead)
-            out_sb = out_pool.tile([P, PAIR * HEADS * QK], F32)
-            out_tiles[r] = out_sb
-            terms = rotate_products(r)
-            if ahead < PAIRS:
-                quantise_pair(ahead)
-            rotate_sum(r, terms)
-            copy_nope(r)
-            store_pair(r)
+        for first in range(0, PAIRS, ROUND):
+            second = first + 1
+            more = first + ROUND < PAIRS
+            multiply_pair(first)
+            group_pair(second)
+            if more:
+                transpose_pair(first + ROUND)
+                transpose_pair(second + ROUND)
+            finish_pair(first, quantise_between=second)
+            multiply_pair(second)
+            if more:
+                group_pair(first + ROUND)
+                quantise_pair(first + ROUND)
+            finish_pair(second, quantise_between=None)

@@ -27,7 +27,8 @@ CHUNK_COLS = HEADS * PART
 ROPE_CHUNK = CHUNKS - 1
 CHUNK_ORDER = (ROPE_CHUNK, 0, 1, 2)
 BANK = 512
-ROUND = 2
+AHEAD = 2
+RUN = 2
 
 FLOPS = 2 * BATCH * SEQ * DIM * HEADS * QK
 
@@ -41,7 +42,7 @@ def tile_mla_pa_t_kernel(tc, x, w, freqs, out):
         const = ctx.enter_context(tc.tile_pool(name="const", bufs=1))
         x_pool = ctx.enter_context(tc.tile_pool(name="x_pool", bufs=PAIRS))
         grouped_pool = ctx.enter_context(tc.tile_pool(name="grouped_pool", bufs=3))
-        code_pool = ctx.enter_context(tc.tile_pool(name="code_pool", bufs=2 * ROUND))
+        code_pool = ctx.enter_context(tc.tile_pool(name="code_pool", bufs=AHEAD + 2))
         term_pool = ctx.enter_context(tc.tile_pool(name="term_pool", bufs=2))
         out_pool = ctx.enter_context(tc.tile_pool(name="out_pool", bufs=6))
         xt_pool = ctx.enter_context(tc.psum_pool(name="xt_pool", bufs=4))
@@ -228,34 +229,29 @@ def tile_mla_pa_t_kernel(tc, x, w, freqs, out):
             width = PAIR * HEADS * QK
             nc.sync.dma_start(out=out_rows[b, :, q * width : (q + 1) * width], in_=out_tiles[r][:])
 
-        def finish_pair(r, quantise_between):
-            out_sb = out_pool.tile([P, PAIR * HEADS * QK], F32)
-            out_tiles[r] = out_sb
-            terms = rotate_products(r)
-            if quantise_between is not None:
-                quantise_pair(quantise_between)
-            rotate_sum(r, terms)
-            copy_nope(r)
-            store_pair(r)
-
         transpose_pair(0)
         group_pair(0)
         prepare_w(0, share_with_scalar=False)
         quantise_pair(0)
         prepare_w(1, share_with_scalar=True)
         transpose_pair(1)
+        group_pair(1)
+        quantise_pair(1)
+        transpose_pair(2)
 
-        for first in range(0, PAIRS, ROUND):
-            second = first + 1
-            more = first + ROUND < PAIRS
-            multiply_pair(first)
-            group_pair(second)
-            if more:
-                transpose_pair(first + ROUND)
-                transpose_pair(second + ROUND)
-            finish_pair(first, quantise_between=second)
-            multiply_pair(second)
-            if more:
-                group_pair(first + ROUND)
-                quantise_pair(first + ROUND)
-            finish_pair(second, quantise_between=None)
+        for r in range(PAIRS):
+            ahead = r + AHEAD
+            if r % RUN == 1:
+                for later in range(ahead, min(ahead + RUN, PAIRS)):
+                    transpose_pair(later)
+            multiply_pair(r)
+            if ahead < PAIRS:
+                group_pair(ahead)
+            out_sb = out_pool.tile([P, PAIR * HEADS * QK], F32)
+            out_tiles[r] = out_sb
+            terms = rotate_products(r)
+            if ahead < PAIRS:
+                quantise_pair(ahead)
+            rotate_sum(r, terms)
+            copy_nope(r)
+            store_pair(r)

from contextlib import ExitStack

import concourse.mybir as mybir
from concourse.masks import make_identity

BF16 = mybir.dt.bfloat16
F32 = mybir.dt.float32
U32 = mybir.dt.uint32
U8 = mybir.dt.uint8
FP8X4 = mybir.dt.float8_e4m3fn_x4
ACT = mybir.ActivationFunctionType
ALU = mybir.AluOpType

P = 128
PACK = 4
BATCH, SEQ, DIM = 4, 1024, 1024
HEADS, NOPE, ROPE = 4, 192, 64
QK = NOPE + ROPE
PASSES = DIM // (P * PACK)
TILES = SEQ // P
PAIR = 2
PAIRS_PER_BATCH = TILES // PAIR
PAIRS = BATCH * PAIRS_PER_BATCH
PART = 64
CHUNKS = QK // PART
CHUNK_COLS = HEADS * PART
ROPE_CHUNK = CHUNKS - 1
CHUNK_ORDER = (ROPE_CHUNK, 0, 1, 2)
BANK = 512
AHEAD = 2
RUN = 2

FLOPS = 2 * BATCH * SEQ * DIM * HEADS * QK


def tile_mla_pa_t_kernel(tc, x, w, freqs, out):
    nc = tc.nc
    x_rows = x.rearrange("b (p i) k -> b p (i k)", i=TILES)
    out_rows = out.rearrange("b (p i) h d -> b p (i h d)", i=TILES)

    with ExitStack() as ctx:
        const = ctx.enter_context(tc.tile_pool(name="const", bufs=1))
        x_pool = ctx.enter_context(tc.tile_pool(name="x_pool", bufs=PAIRS))
        grouped_pool = ctx.enter_context(tc.tile_pool(name="grouped_pool", bufs=3))
        code_pool = ctx.enter_context(tc.tile_pool(name="code_pool", bufs=AHEAD + 2))
        term_pool = ctx.enter_context(tc.tile_pool(name="term_pool", bufs=2))
        out_pool = ctx.enter_context(tc.tile_pool(name="out_pool", bufs=6))
        xt_pool = ctx.enter_context(tc.psum_pool(name="xt_pool", bufs=4))
        acc_pool = ctx.enter_context(tc.psum_pool(name="acc_pool", bufs=4))
        ctx.enter_context(tc.manual_schedule())

        angles = const.tile([P, TILES * ROPE // 2], BF16)
        nc.scalar.dma_start(out=angles[:], in_=freqs.rearrange("(p i) j -> p (i j)", i=TILES))

        w_raw = const.tile([P, PASSES, PACK, DIM], BF16)

        def load_w(g):
            rows = w[g * P * PACK : (g + 1) * P * PACK, :]
            nc.sync.dma_start(
                out=w_raw[:, g].rearrange("p (u e) n -> p u (e n)", u=2),
                in_=rows.rearrange("(u p e) n -> p u (e n)", u=2, e=2),
            )

        x_tiles = {}

        def load_x(r):
            b, q = divmod(r, PAIRS_PER_BATCH)
            x_sb = x_pool.tile([P, PAIR * DIM], BF16)
            nc.sync.dma_start(out=x_sb[:], in_=x_rows[b, :, q * PAIR * DIM : (q + 1) * PAIR * DIM])
            x_tiles[r] = x_sb

        load_w(0)
        load_x(0)
        load_w(1)
        for r in range(1, PAIRS):
            load_x(r)

        ident = const.tile([P, P], F32)
        make_identity(nc, ident[:])

        u_table = const.tile([P, TILES, ROPE], F32)
        v_table = const.tile([P, TILES, ROPE], F32)
        u_cols = u_table[:].rearrange("p i (j e) -> p (i j) e", e=2)
        v_cols = v_table[:].rearrange("p i (j e) -> p (i j) e", e=2)
        half_sin = const.tile([P, TILES * ROPE // 2], F32)
        half_sq = const.tile([P, TILES * ROPE // 2], F32)
        nc.scalar.activation(out=half_sin[:], in_=angles[:], func=ACT.Sin, scale=0.5)
        nc.scalar.activation(out=u_cols[:, :, 1], in_=angles[:], func=ACT.Sin)
        nc.scalar.activation(out=v_cols[:, :, 0], in_=angles[:], func=ACT.Sin, scale=-1.0)
        nc.scalar.activation(out=half_sq[:], in_=half_sin[:], func=ACT.Square)
        nc.scalar.activation(out=u_cols[:, :, 0], in_=half_sq[:], func=ACT.Copy, scale=-2.0, bias=1.0)
        nc.scalar.activation(out=v_cols[:, :, 1], in_=half_sq[:], func=ACT.Copy, scale=-2.0, bias=1.0)

        xt_banks = {}
        grouped_tiles = {}
        x_codes = {}
        x_scales = {}

        def transpose_pair(r):
            words = x_tiles[r][:].bitcast(F32)
            xt_banks[r] = []
            for t in range(PAIR):
                xt = xt_pool.tile([P, BANK], F32)
                for s in range(PACK):
                    col = (t * PACK + s) * P
                    nc.tensor.transpose(
                        out=xt[:, s * P : (s + 1) * P], in_=words[:, col : col + P], identity=ident[:]
                    )
                xt_banks[r].append(xt)

        def group_pair(r):
            grouped = grouped_pool.tile([P, PAIR * DIM], BF16, align_bytes=64)
            grouped_words = grouped[:].bitcast(F32)
            for t in range(PAIR):
                nc.scalar.copy(
                    out=grouped_words[:, t * BANK : (t + 1) * BANK].rearrange(
                        "p (g k u) -> p g k u", g=PASSES, u=2
                    ),
                    in_=xt_banks[r][t][:].rearrange("p (g u k) -> p g k u", g=PASSES, u=2),
                )
            grouped_tiles[r] = grouped

        def quantise_pair(r):
            codes = code_pool.tile([P, PAIR * PASSES * P], U32, align_bytes=64)
            scales = code_pool.tile([P, PAIR * PASSES * P], U8, align_bytes=64)
            nc.vector.quantize_mx(
                out=codes[:].bitcast(FP8X4), scales=scales[:], in_=grouped_tiles[r][:]
            )
            x_codes[r] = codes
            x_scales[r] = scales

        w_grouped = const.tile([P, PASSES, CHUNKS, CHUNK_COLS * PACK], BF16, align_bytes=64)
        w_codes = const.tile([P, PASSES, CHUNKS * CHUNK_COLS], U32, align_bytes=64)
        w_scales = const.tile([P, PASSES, CHUNKS * CHUNK_COLS], U8, align_bytes=64)

        def group_w(g, c, on_scalar):
            if c == ROPE_CHUNK:
                src = w_raw[:, g, :, HEADS * NOPE :].rearrange("p t (h n) -> p h n t", h=HEADS)
            else:
                src = w_raw[:, g, :, : HEADS * NOPE].rearrange(
                    "p t (h c n) -> p c h n t", h=HEADS, n=PART
                )[:, c]
            dst = w_grouped[:, g, c, :].rearrange("p (h n t) -> p h n t", h=HEADS, t=PACK)
            if on_scalar:
                nc.scalar.copy(out=dst, in_=src)
            else:
                nc.vector.tensor_copy(out=dst, in_=src)

        def quantise_w(g, c):
            cols = slice(c * CHUNK_COLS, (c + 1) * CHUNK_COLS)
            nc.vector.quantize_mx(
                out=w_codes[:, g, cols].bitcast(FP8X4),
                scales=w_scales[:, g, cols],
                in_=w_grouped[:, g, c, :],
            )

        def prepare_w(g, share_with_scalar):
            for n, c in enumerate(CHUNK_ORDER):
                group_w(g, c, on_scalar=share_with_scalar and n % 2 == 1)
                if n > 0:
                    quantise_w(g, CHUNK_ORDER[n - 1])
            quantise_w(g, CHUNK_ORDER[-1])

        acc_banks = {}
        out_tiles = {}

        def multiply_pair(r):
            for c in CHUNK_ORDER:
                acc = acc_pool.tile([P, BANK], F32)
                w_cols = slice(c * CHUNK_COLS, (c + 1) * CHUNK_COLS)
                for t in range(PAIR):
                    for g in range(PASSES):
                        x_cols = slice((t * PASSES + g) * P, (t * PASSES + g + 1) * P)
                        nc.tensor.matmul_mx(
                            out=acc[:, t * CHUNK_COLS : (t + 1) * CHUNK_COLS],
                            lhsT=x_codes[r][:, x_cols].bitcast(FP8X4),
                            lhsT_scale=x_scales[r][:, x_cols],
                            rhs=w_codes[:, g, w_cols].bitcast(FP8X4),
                            rhs_scale=w_scales[:, g, w_cols],
                            start=(g == 0),
                            stop=(g == PASSES - 1),
                        )
                acc_banks[r, c] = acc

        full = [P, PAIR, HEADS, ROPE // 2, 2]
        split = "p (t h j e) -> p t h j e"

        def rotate_products(r):
            i0 = (r % PAIRS_PER_BATCH) * PAIR
            pairs = acc_banks[r, ROPE_CHUNK][:].rearrange(split, t=PAIR, h=HEADS, e=2)
            terms = []
            for e, table in enumerate((u_table, v_table)):
                term = term_pool.tile([P, BANK], F32, name="term%d" % e)
                nc.vector.tensor_tensor(
                    out=term[:].rearrange(split, t=PAIR, h=HEADS, e=2),
                    in0=pairs[:, :, :, :, e : e + 1].to_broadcast(full),
                    in1=table[:, i0 : i0 + PAIR, :]
                    .rearrange("p t (j e) -> p t j e", e=2)
                    .unsqueeze(2)
                    .to_broadcast(full),
                    op=ALU.mult,
                )
                terms.append(term)
            return terms

        def out_part(r, c):
            view = out_tiles[r][:].rearrange("p (t h d) -> p t h d", t=PAIR, h=HEADS)
            return view[:, :, :, c * PART : (c + 1) * PART]

        by_head = "p (t h n) -> p t h n"

        def rotate_sum(r, terms):
            nc.vector.tensor_tensor(
                out=out_part(r, ROPE_CHUNK),
                in0=terms[0][:].rearrange(by_head, t=PAIR, h=HEADS),
                in1=terms[1][:].rearrange(by_head, t=PAIR, h=HEADS),
                op=ALU.add,
            )

        def copy_nope(r):
            for c in range(ROPE_CHUNK):
                nc.scalar.copy(
                    out=out_part(r, c),
                    in_=acc_banks[r, c][:].rearrange(by_head, t=PAIR, h=HEADS),
                )

        def store_pair(r):
            b, q = divmod(r, PAIRS_PER_BATCH)
            width = PAIR * HEADS * QK
            nc.sync.dma_start(out=out_rows[b, :, q * width : (q + 1) * width], in_=out_tiles[r][:])

        transpose_pair(0)
        group_pair(0)
        prepare_w(0, share_with_scalar=False)
        quantise_pair(0)
        prepare_w(1, share_with_scalar=True)
        transpose_pair(1)
        group_pair(1)
        quantise_pair(1)
        transpose_pair(2)

        for r in range(PAIRS):
            ahead = r + AHEAD
            if r % RUN == 1:
                for later in range(ahead, min(ahead + RUN, PAIRS)):
                    transpose_pair(later)
            multiply_pair(r)
            if ahead < PAIRS:
                group_pair(ahead)
            out_sb = out_pool.tile([P, PAIR * HEADS * QK], F32)
            out_tiles[r] = out_sb
            terms = rotate_products(r)
            if ahead < PAIRS:
                quantise_pair(ahead)
            rotate_sum(r, terms)
            copy_nope(r)
            store_pair(r)
